import numpy as np
import ml_dtypes


def mxq(x, axis, fmt="e4m3"):
    dtype, down = {"e4m3": (ml_dtypes.float8_e4m3fn, 7), "e5m2": (ml_dtypes.float8_e5m2, 14)}[fmt]
    v = np.moveaxis(np.asarray(x, np.float32).astype(ml_dtypes.bfloat16).astype(np.float64), axis, -1)
    blocks = v.reshape(v.shape[:-1] + (-1, 32))
    amax = np.abs(blocks).max(-1, keepdims=True)
    byte = np.maximum(np.where(amax > 0, np.frexp(amax)[1] - 1 + 127, 0) - down, 1)
    scale = np.exp2(byte - 127.0)
    codes = (blocks / scale).astype(np.float32).astype(dtype).astype(np.float64)
    return np.moveaxis((codes * scale).reshape(v.shape), -1, axis)


WIDE = False


def mx_kscale(k):
    if not WIDE:
        return np.ones(k)
    levels = np.array([10, -10, 5, -5, 0])
    a = np.random.permutation(np.resize(levels, k // 512 * 4)).reshape(k // 512, 4)
    idx = np.arange(k)
    return np.exp2(a[idx // 512, idx % 128 // 32])


BF16 = ml_dtypes.bfloat16


def bf(x):
    return np.asarray(x, np.float32).astype(BF16)


def f64(x):
    return np.asarray(x).astype(np.float64)


B, N, F, DIM, H, DH, D3 = 4, 196, 16, 512, 1, 64, 512
W = H * D3
SCALE = 1.0 / (np.sqrt(DH) * H)
QS = np.sqrt(1.5 / (SCALE * np.sqrt(D3)))


def setup_inputs():
    s, t = mx_kscale(DIM), mx_kscale(D3)
    th = np.tile(t, H)
    return {"x": bf(np.random.standard_normal((B, N * F, DIM)) * s),
            "Wq": bf(np.random.standard_normal((DIM, W)) * QS / np.sqrt(DIM) / s[:, None] * th),
            "bq": bf(np.random.standard_normal(W) * 0.2 * QS * th),
            "k": bf(np.random.standard_normal((B, H, N, F, D3)) * QS / t)}


def reference(x, Wq, bq, k):
    y = (mxq(f64(x), 2, "e4m3") @ mxq(f64(Wq), 0, "e4m3")) + f64(bq)
    q = y.reshape(B, F, N, H, D3).transpose(0, 3, 2, 1, 4)
    s = (mxq(q, 4, "e4m3") @ mxq(f64(k), 4, "e4m3").transpose(0, 1, 2, 4, 3)) * SCALE
    e = np.exp(s - s.max(-1, keepdims=True))
    return e / e.sum(-1, keepdims=True)

@@ -1,0 +1,381 @@
+from contextlib import ExitStack
+
+import concourse.mybir as mybir
+from concourse.masks import make_identity
+
+F32 = mybir.dt.float32
+BF16 = mybir.dt.bfloat16
+U32 = mybir.dt.uint32
+U8 = mybir.dt.uint8
+FP8X4 = mybir.dt.float8_e4m3fn_x4
+ALU = mybir.AluOpType
+ACT = mybir.ActivationFunctionType
+AX = mybir.AxisListType
+
+P = 128
+E = 512
+STEPS = 98
+FLOPS = 2 * 12544 * 512 * 512 + 2 * 784 * 16 * 16 * 512
+BIG = 2.0 ** 100
+
+BLOCKS = [(96, 2)] + [(8 * i, 8) for i in range(12)]
+HALVES = {
+    8: (((0, 4, "S"),), ((4, 2, "S"), (6, 1, "V"), (7, 1, "V"))),
+    2: (((0, 1, "V"),), ((1, 1, "V"),)),
+}
+
+
+def tile_dividedspacetimeattention_pa_t_kernel(tc, x, Wq, bq, k, out):
+    nc = tc.nc
+    nb = len(BLOCKS)
+    xv = x.rearrange("b (q t) e -> (b q) t e", t=STEPS)
+    kv = k.rearrange("b h (j t) g e -> (t g) (b h j) e", j=2, t=STEPS)
+    ov = out.rearrange("b h (j t) f g -> (t f) (b h j) g", j=2, t=STEPS)
+
+    with ExitStack() as ctx:
+        const = ctx.enter_context(tc.tile_pool(name="const", bufs=1))
+        sb = ctx.enter_context(tc.tile_pool(name="sb", bufs=2))
+        ps = ctx.enter_context(tc.psum_pool(name="ps", bufs=1))
+        ctx.enter_context(tc.manual_schedule())
+
+        x_sb = {}
+        k_sb = {}
+        xg = {}
+        kg = {}
+        xc = {}
+        kc = {}
+        qp = {}
+        qg = {}
+        qc = {}
+        s_sb = {}
+        e_sb = {}
+
+        def load(b):
+            t0, T = BLOCKS[b]
+            L = 8 // T
+            xt = sb.tile([P, 8 * E], BF16, name="x_sb", tag="x_sb", bufs=3)
+            nc.sync.dma_start(
+                out=xt[:, 0 : E * T].rearrange("p (t e) -> p t e", e=E),
+                in_=xv[:, t0 : t0 + T, :],
+            )
+            x_sb[b] = xt
+            kt = sb.tile([P, 8 * E], BF16, name="k_sb", tag="k_sb", bufs=3)
+            k3 = kt[:, 0 : E * T].rearrange("p (h e) -> p h e", e=E)
+            rows = kv[16 * t0 : 16 * (t0 + T), :, :].rearrange("r (h l) e -> l r h e", l=L)
+            for l in range(L):
+                nc.sync.dma_start(out=k3[16 * T * l : 16 * T * (l + 1), :, :], in_=rows[l])
+            k_sb[b] = kt
+
+        load(0)
+        wraw = const.tile([P, 4, E], BF16, name="wraw")
+        for u in range(2):
+            nc.sync.dma_start(
+                out=wraw[:, 2 * u : 2 * u + 2, :],
+                in_=Wq[256 * u : 256 * u + 256, :].rearrange("(p e) n -> p e n", e=2),
+            )
+        b_bf = const.tile([P, 4], BF16, name="b_bf")
+        nc.scalar.dma_start(
+            out=b_bf[:].rearrange("p (u e) -> p u e", u=2),
+            in_=bq.rearrange("(u p e) -> p u e", u=2, e=2),
+        )
+        load(1)
+
+        ident = const.tile([P, P], F32, name="ident")
+        make_identity(nc, ident[:])
+        zero = const.tile([P, 8], F32, name="zero")
+        nc.vector.memset(zero[:], 0.0)
+        warm = const.tile([P, 8], F32, name="warm")
+        nc.scalar.activation(out=warm[:], in_=zero[:], func=ACT.Exp)
+
+        perm = const.tile([P, P], F32, name="perm")
+        nc.vector.tensor_copy(
+            out=perm[:].rearrange("p (b j f) -> p b j f", b=4, j=2, f=16),
+            in_=ident[:].rearrange("p (b f j) -> p b j f", b=4, f=16, j=2),
+        )
+        ag = const.tile([P, 4 * P], BF16, name="ag", align_bytes=64)
+        bg = const.tile([P, 4 * P], BF16, name="bg", align_bytes=64)
+        nc.vector.memset(ag[:], 0.0)
+        nc.vector.memset(bg[:], 0.0)
+        slot = ident[:, 0:8].unsqueeze(2).to_broadcast([P, 8, 16])
+        nc.vector.tensor_copy(
+            out=ag[:].rearrange("p (s f j) -> p s f j", s=8, f=16, j=4)[:, :, :, 0], in_=slot
+        )
+        nc.vector.tensor_scalar(
+            out=bg[:].rearrange("p (s f j) -> p s f j", s=8, f=16, j=4)[:, :, :, 0],
+            in0=slot,
+            scalar1=-1.0,
+            scalar2=BIG,
+            op0=ALU.add,
+            op1=ALU.mult,
+        )
+        ac = const.tile([P, P], U32, name="ac", align_bytes=64)
+        asc = const.tile([P, P], U8, name="asc", align_bytes=64)
+        bc = const.tile([P, P], U32, name="bc", align_bytes=64)
+        bsc = const.tile([P, P], U8, name="bsc", align_bytes=64)
+        nc.vector.quantize_mx(out=ac[:].bitcast(FP8X4), scales=asc[:], in_=ag[:])
+        nc.vector.quantize_mx(out=bc[:].bitcast(FP8X4), scales=bsc[:], in_=bg[:])
+
+        b32 = const.tile([P, 4], F32, name="b32")
+        nc.vector.tensor_copy(out=b32[:], in_=b_bf[:])
+        wg = const.tile([P, 4 * E], BF16, name="wg", align_bytes=64)
+        wgv = wg[:].rearrange("p (u e m j) -> p u e m j", u=2, e=2, m=P, j=4)
+        wrv = wraw[:].rearrange("p j (u m e) -> p u e m j", u=2, m=P, e=2)
+        for u in range(2):
+            for e in range(2):
+                nc.vector.tensor_copy(out=wgv[:, u, e], in_=wrv[:, u, e])
+        wc = const.tile([P, E], U32, name="wc", align_bytes=64)
+        ws = const.tile([P, E], U8, name="ws", align_bytes=64)
+        nc.vector.quantize_mx(out=wc[:].bitcast(FP8X4), scales=ws[:], in_=wg[:])
+
+        def tx(b):
+            t0, T = BLOCKS[b]
+            xw = x_sb[b][:].bitcast(F32)
+            g = sb.tile([P, 8 * E], BF16, name="xg", tag="xg", bufs=2, align_bytes=64)
+            gv = g[:].bitcast(F32)[:, 0 : 256 * T].rearrange(
+                "p (c t f u) -> p c t f u", c=8, t=T, f=16, u=2
+            )
+            banks = []
+            for m in range(T // 2):
+                tr = ps.tile([P, 512], F32, name="tr", tag="tr", bufs=4)
+                for s in range(2):
+                    for u in range(2):
+                        c0 = 256 * (2 * m + s) + 128 * u
+                        nc.tensor.transpose(
+                            tr[:, 256 * s + 128 * u : 256 * s + 128 * u + 128],
+                            xw[:, c0 : c0 + 128],
+                            perm[:],
+                        )
+                banks.append(tr)
+            for m in range(T // 2):
+                for s in range(2):
+                    nc.scalar.copy(
+                        out=gv[:, :, 2 * m + s, :, :],
+                        in_=banks[m][:, 256 * s : 256 * s + 256].rearrange(
+                            "p (u c f) -> p c f u", u=2, c=8, f=16
+                        ),
+                    )
+            xg[b] = g
+
+        def tk(b):
+            t0, T = BLOCKS[b]
+            kw = k_sb[b][:].bitcast(F32)
+            g = sb.tile([P, 8 * E], BF16, name="kg", tag="kg", bufs=2, align_bytes=64)
+            gw = g[:].bitcast(F32)
+            banks = []
+            for m in range(T // 2):
+                tr = ps.tile([P, 512], F32, name="tr", tag="tr", bufs=4)
+                for s in range(2):
+                    for u in range(2):
+                        c0 = 256 * (2 * m + s) + 128 * u
+                        nc.tensor.transpose(
+                            tr[:, 256 * s + 128 * u : 256 * s + 128 * u + 128],
+                            kw[:, c0 : c0 + 128],
+                            ident[:],
+                        )
+                banks.append(tr)
+            for m in range(T // 2):
+                nc.scalar.copy(
+                    out=gw[:, 512 * m : 512 * m + 512].rearrange(
+                        "p (s q u) -> p s q u", s=2, q=P, u=2
+                    ),
+                    in_=banks[m][:].rearrange("p (s u q) -> p s q u", s=2, u=2, q=P),
+                )
+            kg[b] = g
+
+        def quant(src, b, store, tag, bufs):
+            t0, T = BLOCKS[b]
+            c = sb.tile([P, 1024], U32, name=tag + "c", tag=tag + "c", bufs=bufs, align_bytes=64)
+            s = sb.tile([P, 1024], U8, name=tag + "s", tag=tag + "s", bufs=bufs, align_bytes=64)
+            nc.vector.quantize_mx(
+                out=c[:, 0 : P * T].bitcast(FP8X4), scales=s[:, 0 : P * T], in_=src[b][:, 0 : E * T]
+            )
+            store[b] = (c, s)
+
+        def m1(b, h):
+            t0, T = BLOCKS[b]
+            c, s = xc[b]
+            if h == 0:
+                qg[b] = sb.tile([P, 8 * E], BF16, name="qg", tag="qg", bufs=2, align_bytes=64)
+            later = []
+            for (g0, ng, kind) in HALVES[T][h]:
+                n = P * ng
+                per = 512 // n
+                if kind == "S":
+                    pl = sb.tile([P, 4, n], BF16, name="qp%d" % ng, tag="qp%d" % ng, bufs=2)
+                    qp[(b, g0)] = pl
+                y = None
+                for j in range(4):
+                    if j % per == 0:
+                        y = ps.tile([P, 512], F32, name="y", tag="y", bufs=3)
+                    o = n * (j % per)
+                    nc.tensor.matmul_mx(
+                        out=y[:, o : o + n],
+                        lhsT=wc[:, P * j : P * j + P].bitcast(FP8X4),
+                        lhsT_scale=ws[:, P * j : P * j + P],
+                        rhs=c[:, P * g0 : P * g0 + n].bitcast(FP8X4),
+                        rhs_scale=s[:, P * g0 : P * g0 + n],
+                        start=True,
+                        stop=True,
+                    )
+                    if kind == "S" and j % per == per - 1:
+                        for jj in range(j - per + 1, j + 1):
+                            oo = n * (jj % per)
+                            nc.scalar.activation(
+                                out=pl[:, jj, :],
+                                in_=y[:, oo : oo + n],
+                                func=ACT.Identity,
+                                bias=b32[:, jj : jj + 1],
+                                scale=1.0,
+                            )
+                if kind == "V":
+                    later.append((g0, y))
+            return later
+
+        def vd(b, later):
+            for (g0, y) in later:
+                nc.vector.tensor_tensor(
+                    out=qg[b][:, E * g0 : E * g0 + E].rearrange("p (q j) -> p q j", j=4),
+                    in0=y[:].rearrange("p (j q) -> p q j", j=4),
+                    in1=b32[:].unsqueeze(1).to_broadcast([P, P, 4]),
+                    op=ALU.add,
+                )
+
+        def rg(b, h):
+            t0, T = BLOCKS[b]
+            for (g0, ng, kind) in HALVES[T][h]:
+                if kind == "S":
+                    nc.vector.tensor_copy(
+                        out=qg[b][:, E * g0 : E * (g0 + ng)].rearrange(
+                            "p (c i j) -> p c j i", i=4, j=4
+                        ),
+                        in_=qp[(b, g0)][:].rearrange("p j (c i) -> p c j i", i=4),
+                    )
+
+        def span(T, h):
+            units = HALVES[T][h]
+            g0 = units[0][0]
+            g1 = units[-1][0] + units[-1][1]
+            return g0, g1
+
+        def qq(b, h):
+            t0, T = BLOCKS[b]
+            g0, g1 = span(T, h)
+            if h == 0:
+                c = sb.tile([P, 1024], U32, name="qc", tag="qc", bufs=2, align_bytes=64)
+                s = sb.tile([P, 1024], U8, name="qs", tag="qs", bufs=2, align_bytes=64)
+                qc[b] = (c, s)
+            c, s = qc[b]
+            nc.vector.quantize_mx(
+                out=c[:, P * g0 : P * g1].bitcast(FP8X4),
+                scales=s[:, P * g0 : P * g1],
+                in_=qg[b][:, E * g0 : E * g1],
+            )
+
+        def m2(b, h):
+            t0, T = BLOCKS[b]
+            g0, g1 = span(T, h)
+            c, s = qc[b]
+            c2, s2 = kc[b]
+            sc = ps.tile([P, 512], F32, name="sc", tag="sc", bufs=1)
+            for g in range(g0, g1):
+                o = P * (g - g0)
+                nc.tensor.matmul_mx(
+                    out=sc[:, o : o + P],
+                    lhsT=c[:, P * g : P * g + P].bitcast(FP8X4),
+                    lhsT_scale=s[:, P * g : P * g + P],
+                    rhs=c2[:, P * g : P * g + P].bitcast(FP8X4),
+                    rhs_scale=s2[:, P * g : P * g + P],
+                    start=True,
+                    stop=False,
+                )
+                nc.tensor.matmul_mx(
+                    out=sc[:, o : o + P],
+                    lhsT=ac[:].bitcast(FP8X4),
+                    lhsT_scale=asc[:],
+                    rhs=bc[:].bitcast(FP8X4),
+                    rhs_scale=bsc[:],
+                    start=False,
+                    stop=True,
+                )
+            return sc
+
+        def red(b, h, sc):
+            t0, T = BLOCKS[b]
+            g0, g1 = span(T, h)
+            if h == 0:
+                s_sb[b] = sb.tile([P, 128], F32, name="s_sb", tag="s_sb", bufs=3)
+            nc.vector.tensor_reduce(
+                out=s_sb[b][:, 16 * g0 : 16 * g1].rearrange("p (l g) -> p l g", g=16),
+                in_=sc[:, 0 : P * (g1 - g0)].rearrange("p (l t g) -> p l g t", t=8, g=16),
+                axis=AX.X,
+                op=ALU.max,
+            )
+
+        def sm1(b):
+            t0, T = BLOCKS[b]
+            s3 = s_sb[b][:, 0 : 16 * T].rearrange("p (l g) -> p l g", g=16)
+            mx = sb.tile([P, 8], F32, name="mx", tag="mx", bufs=2)
+            nc.vector.tensor_reduce(out=mx[:, 0:T], in_=s3, axis=AX.X, op=ALU.max)
+            d = sb.tile([P, 128], F32, name="d_sb", tag="d_sb", bufs=2)
+            nc.vector.tensor_tensor(
+                out=d[:, 0 : 16 * T].rearrange("p (l g) -> p l g", g=16),
+                in0=s3,
+                in1=mx[:, 0:T].unsqueeze(2).to_broadcast([P, T, 16]),
+                op=ALU.subtract,
+            )
+            ex = sb.tile([P, 128], F32, name="e_sb", tag="e_sb", bufs=2)
+            nc.scalar.activation(out=ex[:, 0 : 16 * T], in_=d[:, 0 : 16 * T], func=ACT.Exp, scale=0.125)
+            e_sb[b] = ex
+
+        def sm2(b):
+            t0, T = BLOCKS[b]
+            L = 8 // T
+            e3 = e_sb[b][:, 0 : 16 * T].rearrange("p (l g) -> p l g", g=16)
+            z = sb.tile([P, 8], F32, name="z", tag="z", bufs=2)
+            nc.vector.tensor_reduce(out=z[:, 0:T], in_=e3, axis=AX.X, op=ALU.add)
+            r = sb.tile([P, 8], F32, name="r", tag="r", bufs=2)
+            nc.vector.reciprocal(out=r[:, 0:T], in_=z[:, 0:T])
+            o = sb.tile([P, 128], F32, name="o_sb", tag="o_sb", bufs=3)
+            o3 = o[:, 0 : 16 * T].rearrange("p (l g) -> p l g", g=16)
+            nc.vector.tensor_tensor(
+                out=o3, in0=e3, in1=r[:, 0:T].unsqueeze(2).to_broadcast([P, T, 16]), op=ALU.mult
+            )
+            rows = ov[16 * t0 : 16 * (t0 + T), :, :].rearrange("r (h l) g -> l r h g", l=L)
+            for l in range(L):
+                nc.sync.dma_start(out=rows[l], in_=o3[16 * T * l : 16 * T * (l + 1), :, :])
+
+        def ok(b):
+            return 0 <= b < nb
+
+        for n in range(nb + 4):
+            if ok(n + 2) and n + 2 >= 2:
+                load(n + 2)
+            if ok(n):
+                tx(n)
+            sc = m2(n - 2, 0) if ok(n - 2) else None
+            later = m1(n - 1, 0) if ok(n - 1) else []
+            if ok(n - 1):
+                quant(kg, n - 1, kc, "k", 3)
+            if ok(n - 2):
+                rg(n - 2, 1)
+                red(n - 2, 0, sc)
+                qq(n - 2, 1)
+            if ok(n - 1):
+                vd(n - 1, later)
+            if ok(n - 3):
+                sm1(n - 3)
+            if ok(n):
+                tk(n)
+            sc = m2(n - 2, 1) if ok(n - 2) else None
+            later = m1(n - 1, 1) if ok(n - 1) else []
+            if ok(n):
+                quant(xg, n, xc, "x", 2)
+            if ok(n - 1):
+                rg(n - 1, 0)
+            if ok(n - 2):
+                red(n - 2, 1, sc)
+            if ok(n - 1):
+                qq(n - 1, 0)
+                vd(n - 1, later)
+            if ok(n - 3):
+                sm2(n - 3)

@@ -18,9 +18,10 @@ STEPS = 98
 FLOPS = 2 * 12544 * 512 * 512 + 2 * 784 * 16 * 16 * 512
 BIG = 2.0 ** 100
 
-BLOCKS = [(96, 2)] + [(8 * i, 8) for i in range(12)]
+BLOCKS = [(0, 2), (2, 4)] + [(6 + 8 * i, 8) for i in range(11)] + [(94, 4)]
 HALVES = {
     8: (((0, 4, "S"),), ((4, 2, "S"), (6, 1, "V"), (7, 1, "V"))),
+    4: (((0, 2, "S"),), ((2, 1, "V"), (3, 1, "V"))),
     2: (((0, 1, "V"),), ((1, 1, "V"),)),
 }
 
@@ -36,7 +37,6 @@ def tile_dividedspacetimeattention_pa_t_kernel(tc, x, Wq, bq, k, out):
         const = ctx.enter_context(tc.tile_pool(name="const", bufs=1))
         sb = ctx.enter_context(tc.tile_pool(name="sb", bufs=2))
         ps = ctx.enter_context(tc.psum_pool(name="ps", bufs=1))
-        ctx.enter_context(tc.manual_schedule())
 
         x_sb = {}
         k_sb = {}
@@ -132,28 +132,22 @@ def tile_dividedspacetimeattention_pa_t_kernel(tc, x, Wq, bq, k, out):
             xw = x_sb[b][:].bitcast(F32)
             g = sb.tile([P, 8 * E], BF16, name="xg", tag="xg", bufs=2, align_bytes=64)
             gv = g[:].bitcast(F32)[:, 0 : 256 * T].rearrange(
-                "p (c t f u) -> p c t f u", c=8, t=T, f=16, u=2
+                "p (c m q u) -> p c m q u", c=8, m=T // 2, q=32, u=2
             )
             banks = []
             for m in range(T // 2):
                 tr = ps.tile([P, 512], F32, name="tr", tag="tr", bufs=4)
+                trv = tr[:].rearrange("p (u c s f) -> p u c s f", u=2, c=8, s=2, f=16)
                 for s in range(2):
                     for u in range(2):
                         c0 = 256 * (2 * m + s) + 128 * u
-                        nc.tensor.transpose(
-                            tr[:, 256 * s + 128 * u : 256 * s + 128 * u + 128],
-                            xw[:, c0 : c0 + 128],
-                            perm[:],
-                        )
+                        nc.tensor.transpose(trv[:, u, :, s, :], xw[:, c0 : c0 + 128], perm[:])
                 banks.append(tr)
             for m in range(T // 2):
-                for s in range(2):
-                    nc.scalar.copy(
-                        out=gv[:, :, 2 * m + s, :, :],
-                        in_=banks[m][:, 256 * s : 256 * s + 256].rearrange(
-                            "p (u c f) -> p c f u", u=2, c=8, f=16
-                        ),
-                    )
+                nc.scalar.copy(
+                    out=gv[:, :, m, :, :],
+                    in_=banks[m][:].rearrange("p (u c q) -> p c q u", u=2, c=8, q=32),
+                )
             xg[b] = g
 
         def tk(b):
@@ -317,7 +311,7 @@ def tile_dividedspacetimeattention_pa_t_kernel(tc, x, Wq, bq, k, out):
             mx = sb.tile([P, 8], F32, name="mx", tag="mx", bufs=2)
             nc.vector.tensor_reduce(out=mx[:, 0:T], in_=s3, axis=AX.X, op=ALU.max)
             d = sb.tile([P, 128], F32, name="d_sb", tag="d_sb", bufs=2)
-            nc.vector.tensor_tensor(
+            nc.gpsimd.tensor_tensor(
                 out=d[:, 0 : 16 * T].rearrange("p (l g) -> p l g", g=16),
                 in0=s3,
                 in1=mx[:, 0:T].unsqueeze(2).to_broadcast([P, T, 16]),
@@ -337,7 +331,7 @@ def tile_dividedspacetimeattention_pa_t_kernel(tc, x, Wq, bq, k, out):
             nc.vector.reciprocal(out=r[:, 0:T], in_=z[:, 0:T])
             o = sb.tile([P, 128], F32, name="o_sb", tag="o_sb", bufs=3)
             o3 = o[:, 0 : 16 * T].rearrange("p (l g) -> p l g", g=16)
-            nc.vector.tensor_tensor(
+            nc.gpsimd.tensor_tensor(
                 out=o3, in0=e3, in1=r[:, 0:T].unsqueeze(2).to_broadcast([P, T, 16]), op=ALU.mult
             )
             rows = ov[16 * t0 : 16 * (t0 + T), :, :].rearrange("r (h l) g -> l r h g", l=L)

@@ -19,11 +19,6 @@ FLOPS = 2 * 12544 * 512 * 512 + 2 * 784 * 16 * 16 * 512
 BIG = 2.0 ** 100
 
 BLOCKS = [(0, 2), (2, 4)] + [(6 + 8 * i, 8) for i in range(11)] + [(94, 4)]
-HALVES = {
-    8: (((0, 4, "S"),), ((4, 2, "S"), (6, 1, "V"), (7, 1, "V"))),
-    4: (((0, 2, "S"),), ((2, 1, "V"), (3, 1, "V"))),
-    2: (((0, 1, "V"),), ((1, 1, "V"),)),
-}
 
 
 def tile_dividedspacetimeattention_pa_t_kernel(tc, x, Wq, bq, k, out):
@@ -37,6 +32,7 @@ def tile_dividedspacetimeattention_pa_t_kernel(tc, x, Wq, bq, k, out):
         const = ctx.enter_context(tc.tile_pool(name="const", bufs=1))
         sb = ctx.enter_context(tc.tile_pool(name="sb", bufs=2))
         ps = ctx.enter_context(tc.psum_pool(name="ps", bufs=1))
+        ctx.enter_context(tc.manual_schedule())
 
         x_sb = {}
         k_sb = {}
@@ -48,7 +44,12 @@ def tile_dividedspacetimeattention_pa_t_kernel(tc, x, Wq, bq, k, out):
         qg = {}
         qc = {}
         s_sb = {}
+        d_sb = {}
         e_sb = {}
+        r_sb = {}
+        tr_of = {}
+        y_of = {}
+        sc_of = {}
 
         def load(b):
             t0, T = BLOCKS[b]
@@ -127,37 +128,36 @@ def tile_dividedspacetimeattention_pa_t_kernel(tc, x, Wq, bq, k, out):
         ws = const.tile([P, E], U8, name="ws", align_bytes=64)
         nc.vector.quantize_mx(out=wc[:].bitcast(FP8X4), scales=ws[:], in_=wg[:])
 
-        def tx(b):
+        def t_x(b):
             t0, T = BLOCKS[b]
             xw = x_sb[b][:].bitcast(F32)
-            g = sb.tile([P, 8 * E], BF16, name="xg", tag="xg", bufs=2, align_bytes=64)
-            gv = g[:].bitcast(F32)[:, 0 : 256 * T].rearrange(
-                "p (c m q u) -> p c m q u", c=8, m=T // 2, q=32, u=2
-            )
-            banks = []
             for m in range(T // 2):
-                tr = ps.tile([P, 512], F32, name="tr", tag="tr", bufs=4)
+                tr = ps.tile([P, 512], F32, name="tr", tag="tr", bufs=3)
                 trv = tr[:].rearrange("p (u c s f) -> p u c s f", u=2, c=8, s=2, f=16)
                 for s in range(2):
                     for u in range(2):
                         c0 = 256 * (2 * m + s) + 128 * u
                         nc.tensor.transpose(trv[:, u, :, s, :], xw[:, c0 : c0 + 128], perm[:])
-                banks.append(tr)
+                tr_of[("x", b, m)] = tr
+
+        def c_x(b):
+            t0, T = BLOCKS[b]
+            g = sb.tile([P, 8 * E], BF16, name="xg", tag="xg", bufs=2, align_bytes=64)
+            gv = g[:].bitcast(F32)[:, 0 : 256 * T].rearrange(
+                "p (c m q u) -> p c m q u", c=8, m=T // 2, q=32, u=2
+            )
             for m in range(T // 2):
                 nc.scalar.copy(
                     out=gv[:, :, m, :, :],
-                    in_=banks[m][:].rearrange("p (u c q) -> p c q u", u=2, c=8, q=32),
+                    in_=tr_of[("x", b, m)][:].rearrange("p (u c q) -> p c q u", u=2, c=8, q=32),
                 )
             xg[b] = g
 
-        def tk(b):
+        def t_k(b):
             t0, T = BLOCKS[b]
             kw = k_sb[b][:].bitcast(F32)
-            g = sb.tile([P, 8 * E], BF16, name="kg", tag="kg", bufs=2, align_bytes=64)
-            gw = g[:].bitcast(F32)
-            banks = []
             for m in range(T // 2):
-                tr = ps.tile([P, 512], F32, name="tr", tag="tr", bufs=4)
+                tr = ps.tile([P, 512], F32, name="tr", tag="tr", bufs=3)
                 for s in range(2):
                     for u in range(2):
                         c0 = 256 * (2 * m + s) + 128 * u
@@ -166,13 +166,18 @@ def tile_dividedspacetimeattention_pa_t_kernel(tc, x, Wq, bq, k, out):
                             kw[:, c0 : c0 + 128],
                             ident[:],
                         )
-                banks.append(tr)
+                tr_of[("k", b, m)] = tr
+
+        def c_k(b):
+            t0, T = BLOCKS[b]
+            g = sb.tile([P, 8 * E], BF16, name="kg", tag="kg", bufs=2, align_bytes=64)
+            gw = g[:].bitcast(F32)
             for m in range(T // 2):
                 nc.scalar.copy(
                     out=gw[:, 512 * m : 512 * m + 512].rearrange(
                         "p (s q u) -> p s q u", s=2, q=P, u=2
                     ),
-                    in_=banks[m][:].rearrange("p (s u q) -> p s q u", s=2, u=2, q=P),
+                    in_=tr_of[("k", b, m)][:].rearrange("p (s u q) -> p s q u", s=2, u=2, q=P),
                 )
             kg[b] = g
 
@@ -185,96 +190,80 @@ def tile_dividedspacetimeattention_pa_t_kernel(tc, x, Wq, bq, k, out):
             )
             store[b] = (c, s)
 
-        def m1(b, h):
-            t0, T = BLOCKS[b]
+        def m1_pass(b, y, o, j, g0, n):
             c, s = xc[b]
-            if h == 0:
-                qg[b] = sb.tile([P, 8 * E], BF16, name="qg", tag="qg", bufs=2, align_bytes=64)
-            later = []
-            for (g0, ng, kind) in HALVES[T][h]:
-                n = P * ng
-                per = 512 // n
-                if kind == "S":
-                    pl = sb.tile([P, 4, n], BF16, name="qp%d" % ng, tag="qp%d" % ng, bufs=2)
-                    qp[(b, g0)] = pl
-                y = None
-                for j in range(4):
-                    if j % per == 0:
-                        y = ps.tile([P, 512], F32, name="y", tag="y", bufs=3)
-                    o = n * (j % per)
-                    nc.tensor.matmul_mx(
-                        out=y[:, o : o + n],
-                        lhsT=wc[:, P * j : P * j + P].bitcast(FP8X4),
-                        lhsT_scale=ws[:, P * j : P * j + P],
-                        rhs=c[:, P * g0 : P * g0 + n].bitcast(FP8X4),
-                        rhs_scale=s[:, P * g0 : P * g0 + n],
-                        start=True,
-                        stop=True,
-                    )
-                    if kind == "S" and j % per == per - 1:
-                        for jj in range(j - per + 1, j + 1):
-                            oo = n * (jj % per)
-                            nc.scalar.activation(
-                                out=pl[:, jj, :],
-                                in_=y[:, oo : oo + n],
-                                func=ACT.Identity,
-                                bias=b32[:, jj : jj + 1],
-                                scale=1.0,
-                            )
-                if kind == "V":
-                    later.append((g0, y))
-            return later
+            nc.tensor.matmul_mx(
+                out=y[:, o : o + n],
+                lhsT=wc[:, P * j : P * j + P].bitcast(FP8X4),
+                lhsT_scale=ws[:, P * j : P * j + P],
+                rhs=c[:, P * g0 : P * g0 + n].bitcast(FP8X4),
+                rhs_scale=s[:, P * g0 : P * g0 + n],
+                start=True,
+                stop=True,
+            )
 
-        def vd(b, later):
-            for (g0, y) in later:
+        def m1s(b):
+            t0, T = BLOCKS[b]
+            n = P * (T // 2)
+            per = 512 // n
+            pl = sb.tile([P, 4, 512], BF16, name="qp", tag="qp", bufs=2)
+            y = None
+            for j in range(4):
+                if j % per == 0:
+                    y = ps.tile([P, 512], F32, name="y", tag="y", bufs=3)
+                m1_pass(b, y, n * (j % per), j, 0, n)
+                if j % per == per - 1:
+                    for jj in range(j - per + 1, j + 1):
+                        oo = n * (jj % per)
+                        nc.scalar.activation(
+                            out=pl[:, jj, 0:n],
+                            in_=y[:, oo : oo + n],
+                            func=ACT.Identity,
+                            bias=b32[:, jj : jj + 1],
+                            scale=1.0,
+                        )
+            qp[b] = pl
+
+        def rg(b):
+            t0, T = BLOCKS[b]
+            for g in range(T // 2):
+                nc.gpsimd.tensor_scalar(
+                    out=qg[b][:, E * g : E * g + E].rearrange("p (q j) -> p q j", j=4),
+                    in0=qp[b][:, :, P * g : P * g + P].rearrange("p j q -> p q j"),
+                    scalar1=1.0,
+                    scalar2=0.0,
+                    op0=ALU.mult,
+                    op1=ALU.add,
+                )
+
+        def m1v(b):
+            t0, T = BLOCKS[b]
+            qg[b] = sb.tile([P, 8 * E], BF16, name="qg", tag="qg", bufs=3, align_bytes=64)
+            for g in range(T // 2, T):
+                y = ps.tile([P, 512], F32, name="y", tag="y", bufs=3)
+                for j in range(4):
+                    m1_pass(b, y, P * j, j, g, P)
+                y_of[(b, g)] = y
+
+        def vd(b):
+            t0, T = BLOCKS[b]
+            for g in range(T // 2, T):
                 nc.vector.tensor_tensor(
-                    out=qg[b][:, E * g0 : E * g0 + E].rearrange("p (q j) -> p q j", j=4),
-                    in0=y[:].rearrange("p (j q) -> p q j", j=4),
+                    out=qg[b][:, E * g : E * g + E].rearrange("p (q j) -> p q j", j=4),
+                    in0=y_of[(b, g)][:].rearrange("p (j q) -> p q j", j=4),
                     in1=b32[:].unsqueeze(1).to_broadcast([P, P, 4]),
                     op=ALU.add,
                 )
 
-        def rg(b, h):
-            t0, T = BLOCKS[b]
-            for (g0, ng, kind) in HALVES[T][h]:
-                if kind == "S":
-                    nc.vector.tensor_copy(
-                        out=qg[b][:, E * g0 : E * (g0 + ng)].rearrange(
-                            "p (c i j) -> p c j i", i=4, j=4
-                        ),
-                        in_=qp[(b, g0)][:].rearrange("p j (c i) -> p c j i", i=4),
-                    )
-
-        def span(T, h):
-            units = HALVES[T][h]
-            g0 = units[0][0]
-            g1 = units[-1][0] + units[-1][1]
-            return g0, g1
-
-        def qq(b, h):
-            t0, T = BLOCKS[b]
-            g0, g1 = span(T, h)
-            if h == 0:
-                c = sb.tile([P, 1024], U32, name="qc", tag="qc", bufs=2, align_bytes=64)
-                s = sb.tile([P, 1024], U8, name="qs", tag="qs", bufs=2, align_bytes=64)
-                qc[b] = (c, s)
-            c, s = qc[b]
-            nc.vector.quantize_mx(
-                out=c[:, P * g0 : P * g1].bitcast(FP8X4),
-                scales=s[:, P * g0 : P * g1],
-                in_=qg[b][:, E * g0 : E * g1],
-            )
-
         def m2(b, h):
             t0, T = BLOCKS[b]
-            g0, g1 = span(T, h)
             c, s = qc[b]
             c2, s2 = kc[b]
-            sc = ps.tile([P, 512], F32, name="sc", tag="sc", bufs=1)
-            for g in range(g0, g1):
-                o = P * (g - g0)
+            sc = ps.tile([P, 512], F32, name="sc", tag="sc", bufs=2)
+            for i in range(T // 2):
+                g = h * (T // 2) + i
                 nc.tensor.matmul_mx(
-                    out=sc[:, o : o + P],
+                    out=sc[:, P * i : P * i + P],
                     lhsT=c[:, P * g : P * g + P].bitcast(FP8X4),
                     lhsT_scale=s[:, P * g : P * g + P],
                     rhs=c2[:, P * g : P * g + P].bitcast(FP8X4),
@@ -283,7 +272,7 @@ def tile_dividedspacetimeattention_pa_t_kernel(tc, x, Wq, bq, k, out):
                     stop=False,
                 )
                 nc.tensor.matmul_mx(
-                    out=sc[:, o : o + P],
+                    out=sc[:, P * i : P * i + P],
                     lhsT=ac[:].bitcast(FP8X4),
                     lhsT_scale=asc[:],
                     rhs=bc[:].bitcast(FP8X4),
@@ -291,48 +280,62 @@ def tile_dividedspacetimeattention_pa_t_kernel(tc, x, Wq, bq, k, out):
                     start=False,
                     stop=True,
                 )
-            return sc
+            sc_of[(b, h)] = sc
 
-        def red(b, h, sc):
+        def red(b, h):
             t0, T = BLOCKS[b]
-            g0, g1 = span(T, h)
+            w = T // 2
             if h == 0:
-                s_sb[b] = sb.tile([P, 128], F32, name="s_sb", tag="s_sb", bufs=3)
+                s_sb[b] = sb.tile([P, 128], F32, name="s_sb", tag="s_sb", bufs=2)
             nc.vector.tensor_reduce(
-                out=s_sb[b][:, 16 * g0 : 16 * g1].rearrange("p (l g) -> p l g", g=16),
-                in_=sc[:, 0 : P * (g1 - g0)].rearrange("p (l t g) -> p l g t", t=8, g=16),
+                out=s_sb[b][:, 16 * w * h : 16 * w * (h + 1)].rearrange("p (l g) -> p l g", g=16),
+                in_=sc_of[(b, h)][:, 0 : P * w].rearrange("p (l t g) -> p l g t", t=8, g=16),
                 axis=AX.X,
                 op=ALU.max,
             )
 
-        def sm1(b):
+        def shift(b):
             t0, T = BLOCKS[b]
             s3 = s_sb[b][:, 0 : 16 * T].rearrange("p (l g) -> p l g", g=16)
             mx = sb.tile([P, 8], F32, name="mx", tag="mx", bufs=2)
             nc.vector.tensor_reduce(out=mx[:, 0:T], in_=s3, axis=AX.X, op=ALU.max)
             d = sb.tile([P, 128], F32, name="d_sb", tag="d_sb", bufs=2)
-            nc.gpsimd.tensor_tensor(
+            nc.vector.tensor_tensor(
                 out=d[:, 0 : 16 * T].rearrange("p (l g) -> p l g", g=16),
                 in0=s3,
                 in1=mx[:, 0:T].unsqueeze(2).to_broadcast([P, T, 16]),
                 op=ALU.subtract,
             )
+            d_sb[b] = d
+
+        def expo(b):
+            t0, T = BLOCKS[b]
             ex = sb.tile([P, 128], F32, name="e_sb", tag="e_sb", bufs=2)
-            nc.scalar.activation(out=ex[:, 0 : 16 * T], in_=d[:, 0 : 16 * T], func=ACT.Exp, scale=0.125)
+            nc.scalar.activation(
+                out=ex[:, 0 : 16 * T], in_=d_sb[b][:, 0 : 16 * T], func=ACT.Exp, scale=0.125
+            )
             e_sb[b] = ex
 
-        def sm2(b):
+        def total(b):
             t0, T = BLOCKS[b]
-            L = 8 // T
             e3 = e_sb[b][:, 0 : 16 * T].rearrange("p (l g) -> p l g", g=16)
             z = sb.tile([P, 8], F32, name="z", tag="z", bufs=2)
             nc.vector.tensor_reduce(out=z[:, 0:T], in_=e3, axis=AX.X, op=ALU.add)
             r = sb.tile([P, 8], F32, name="r", tag="r", bufs=2)
             nc.vector.reciprocal(out=r[:, 0:T], in_=z[:, 0:T])
+            r_sb[b] = r
+
+        def finish(b):
+            t0, T = BLOCKS[b]
+            L = 8 // T
+            e3 = e_sb[b][:, 0 : 16 * T].rearrange("p (l g) -> p l g", g=16)
             o = sb.tile([P, 128], F32, name="o_sb", tag="o_sb", bufs=3)
             o3 = o[:, 0 : 16 * T].rearrange("p (l g) -> p l g", g=16)
             nc.gpsimd.tensor_tensor(
-                out=o3, in0=e3, in1=r[:, 0:T].unsqueeze(2).to_broadcast([P, T, 16]), op=ALU.mult
+                out=o3,
+                in0=e3,
+                in1=r_sb[b][:, 0:T].unsqueeze(2).to_broadcast([P, T, 16]),
+                op=ALU.mult,
             )
             rows = ov[16 * t0 : 16 * (t0 + T), :, :].rearrange("r (h l) g -> l r h g", l=L)
             for l in range(L):
@@ -341,35 +344,42 @@ def tile_dividedspacetimeattention_pa_t_kernel(tc, x, Wq, bq, k, out):
         def ok(b):
             return 0 <= b < nb
 
-        for n in range(nb + 4):
-            if ok(n + 2) and n + 2 >= 2:
-                load(n + 2)
-            if ok(n):
-                tx(n)
-            sc = m2(n - 2, 0) if ok(n - 2) else None
-            later = m1(n - 1, 0) if ok(n - 1) else []
-            if ok(n - 1):
-                quant(kg, n - 1, kc, "k", 3)
-            if ok(n - 2):
-                rg(n - 2, 1)
-                red(n - 2, 0, sc)
-                qq(n - 2, 1)
-            if ok(n - 1):
-                vd(n - 1, later)
-            if ok(n - 3):
-                sm1(n - 3)
-            if ok(n):
-                tk(n)
-            sc = m2(n - 2, 1) if ok(n - 2) else None
-            later = m1(n - 1, 1) if ok(n - 1) else []
-            if ok(n):
-                quant(xg, n, xc, "x", 2)
-            if ok(n - 1):
-                rg(n - 1, 0)
-            if ok(n - 2):
-                red(n - 2, 1, sc)
-            if ok(n - 1):
-                qq(n - 1, 0)
-                vd(n - 1, later)
-            if ok(n - 3):
-                sm2(n - 3)
+        t_x(0)
+        c_x(0)
+        t_k(0)
+        c_k(0)
+        for i in range(nb + 4):
+            if ok(i + 2):
+                load(i + 2)
+            if ok(i - 2):
+                quant(qg, i - 2, qc, "q", 2)
+            if ok(i - 1):
+                m1s(i - 1)
+            if ok(i - 2):
+                m2(i - 2, 0)
+                m2(i - 2, 1)
+            if ok(i):
+                quant(xg, i, xc, "x", 2)
+                quant(kg, i, kc, "k", 3)
+            if ok(i - 3):
+                expo(i - 3)
+            if ok(i + 1):
+                t_x(i + 1)
+                c_x(i + 1)
+            if ok(i - 3):
+                total(i - 3)
+                finish(i - 3)
+            if ok(i - 1):
+                rg(i - 1)
+            if ok(i):
+                m1v(i)
+            if ok(i - 2):
+                red(i - 2, 0)
+            if ok(i + 1):
+                t_k(i + 1)
+                c_k(i + 1)
+            if ok(i):
+                vd(i)
+            if ok(i - 2):
+                red(i - 2, 1)
+                shift(i - 2)

@@ -19,6 +19,7 @@ FLOPS = 2 * 12544 * 512 * 512 + 2 * 784 * 16 * 16 * 512
 BIG = 2.0 ** 100
 
 BLOCKS = [(0, 2), (2, 4)] + [(6 + 8 * i, 8) for i in range(11)] + [(94, 4)]
+UNITS = {8: ((0, 4), (4, 2), (6, 7)), 4: ((0, 2), None, (2, 3)), 2: ((0, 1), None, (1,))}
 
 
 def tile_dividedspacetimeattention_pa_t_kernel(tc, x, Wq, bq, k, out):
@@ -128,61 +129,55 @@ def tile_dividedspacetimeattention_pa_t_kernel(tc, x, Wq, bq, k, out):
         ws = const.tile([P, E], U8, name="ws", align_bytes=64)
         nc.vector.quantize_mx(out=wc[:].bitcast(FP8X4), scales=ws[:], in_=wg[:])
 
-        def t_x(b):
-            t0, T = BLOCKS[b]
-            xw = x_sb[b][:].bitcast(F32)
-            for m in range(T // 2):
-                tr = ps.tile([P, 512], F32, name="tr", tag="tr", bufs=3)
-                trv = tr[:].rearrange("p (u c s f) -> p u c s f", u=2, c=8, s=2, f=16)
-                for s in range(2):
-                    for u in range(2):
-                        c0 = 256 * (2 * m + s) + 128 * u
-                        nc.tensor.transpose(trv[:, u, :, s, :], xw[:, c0 : c0 + 128], perm[:])
-                tr_of[("x", b, m)] = tr
+        def size(b):
+            return BLOCKS[b][1]
 
-        def c_x(b):
-            t0, T = BLOCKS[b]
-            g = sb.tile([P, 8 * E], BF16, name="xg", tag="xg", bufs=2, align_bytes=64)
-            gv = g[:].bitcast(F32)[:, 0 : 256 * T].rearrange(
-                "p (c m q u) -> p c m q u", c=8, m=T // 2, q=32, u=2
-            )
-            for m in range(T // 2):
+        def tp(b, w, m):
+            T = size(b)
+            if m >= T // 2:
+                return
+            tr = ps.tile([P, 512], F32, name="tr", tag="tr", bufs=4)
+            if w == "x":
+                src = x_sb[b][:].bitcast(F32)
+                trv = tr[:].rearrange("p (u c s f) -> p u c s f", u=2, c=8, s=2, f=16)
+            else:
+                src = k_sb[b][:].bitcast(F32)
+            for s in range(2):
+                for u in range(2):
+                    c0 = 256 * (2 * m + s) + 128 * u
+                    if w == "x":
+                        nc.tensor.transpose(trv[:, u, :, s, :], src[:, c0 : c0 + 128], perm[:])
+                    else:
+                        o = 256 * s + 128 * u
+                        nc.tensor.transpose(tr[:, o : o + 128], src[:, c0 : c0 + 128], ident[:])
+            tr_of[(w, b, m)] = tr
+
+        def cp(b, w, m):
+            T = size(b)
+            if m >= T // 2:
+                return
+            if w == "x":
+                if m == 0:
+                    xg[b] = sb.tile([P, 8 * E], BF16, name="xg", tag="xg", bufs=2, align_bytes=64)
+                gv = xg[b][:].bitcast(F32)[:, 0 : 256 * T].rearrange(
+                    "p (c m q u) -> p c m q u", c=8, m=T // 2, q=32, u=2
+                )
                 nc.scalar.copy(
                     out=gv[:, :, m, :, :],
-                    in_=tr_of[("x", b, m)][:].rearrange("p (u c q) -> p c q u", u=2, c=8, q=32),
+                    in_=tr_of[(w, b, m)][:].rearrange("p (u c q) -> p c q u", u=2, c=8, q=32),
                 )
-            xg[b] = g
-
-        def t_k(b):
-            t0, T = BLOCKS[b]
-            kw = k_sb[b][:].bitcast(F32)
-            for m in range(T // 2):
-                tr = ps.tile([P, 512], F32, name="tr", tag="tr", bufs=3)
-                for s in range(2):
-                    for u in range(2):
-                        c0 = 256 * (2 * m + s) + 128 * u
-                        nc.tensor.transpose(
-                            tr[:, 256 * s + 128 * u : 256 * s + 128 * u + 128],
-                            kw[:, c0 : c0 + 128],
-                            ident[:],
-                        )
-                tr_of[("k", b, m)] = tr
-
-        def c_k(b):
-            t0, T = BLOCKS[b]
-            g = sb.tile([P, 8 * E], BF16, name="kg", tag="kg", bufs=2, align_bytes=64)
-            gw = g[:].bitcast(F32)
-            for m in range(T // 2):
+            else:
+                if m == 0:
+                    kg[b] = sb.tile([P, 8 * E], BF16, name="kg", tag="kg", bufs=2, align_bytes=64)
                 nc.scalar.copy(
-                    out=gw[:, 512 * m : 512 * m + 512].rearrange(
+                    out=kg[b][:].bitcast(F32)[:, 512 * m : 512 * m + 512].rearrange(
                         "p (s q u) -> p s q u", s=2, q=P, u=2
                     ),
-                    in_=tr_of[("k", b, m)][:].rearrange("p (s u q) -> p s q u", s=2, u=2, q=P),
+                    in_=tr_of[(w, b, m)][:].rearrange("p (s u q) -> p s q u", s=2, u=2, q=P),
                 )
-            kg[b] = g
 
         def quant(src, b, store, tag, bufs):
-            t0, T = BLOCKS[b]
+            T = size(b)
             c = sb.tile([P, 1024], U32, name=tag + "c", tag=tag + "c", bufs=bufs, align_bytes=64)
             s = sb.tile([P, 1024], U8, name=tag + "s", tag=tag + "s", bufs=bufs, align_bytes=64)
             nc.vector.quantize_mx(
@@ -202,66 +197,76 @@ def tile_dividedspacetimeattention_pa_t_kernel(tc, x, Wq, bq, k, out):
                 stop=True,
             )
 
-        def m1s(b):
-            t0, T = BLOCKS[b]
-            n = P * (T // 2)
+        def m1s(b, unit, js):
+            g0, ng = unit
+            n = P * ng
             per = 512 // n
-            pl = sb.tile([P, 4, 512], BF16, name="qp", tag="qp", bufs=2)
-            y = None
-            for j in range(4):
+            for j in js:
                 if j % per == 0:
-                    y = ps.tile([P, 512], F32, name="y", tag="y", bufs=3)
-                m1_pass(b, y, n * (j % per), j, 0, n)
-                if j % per == per - 1:
-                    for jj in range(j - per + 1, j + 1):
-                        oo = n * (jj % per)
-                        nc.scalar.activation(
-                            out=pl[:, jj, 0:n],
-                            in_=y[:, oo : oo + n],
-                            func=ACT.Identity,
-                            bias=b32[:, jj : jj + 1],
-                            scale=1.0,
-                        )
-            qp[b] = pl
+                    y_of[(b, g0, j // per)] = ps.tile([P, 512], F32, name="y", tag="y", bufs=3)
+                m1_pass(b, y_of[(b, g0, j // per)], n * (j % per), j, g0, n)
 
-        def rg(b):
-            t0, T = BLOCKS[b]
-            for g in range(T // 2):
-                nc.gpsimd.tensor_scalar(
-                    out=qg[b][:, E * g : E * g + E].rearrange("p (q j) -> p q j", j=4),
-                    in0=qp[b][:, :, P * g : P * g + P].rearrange("p j q -> p q j"),
-                    scalar1=1.0,
-                    scalar2=0.0,
-                    op0=ALU.mult,
-                    op1=ALU.add,
+        def act(b, unit, js):
+            g0, ng = unit
+            n = P * ng
+            per = 512 // n
+            for j in js:
+                if j == 0:
+                    qp[(b, g0)] = sb.tile([P, 4, n], BF16, name="qp%d" % ng, tag="qp%d" % ng, bufs=2)
+                o = n * (j % per)
+                nc.scalar.activation(
+                    out=qp[(b, g0)][:, j, :],
+                    in_=y_of[(b, g0, j // per)][:, o : o + n],
+                    func=ACT.Identity,
+                    bias=b32[:, j : j + 1],
+                    scale=1.0,
                 )
 
-        def m1v(b):
-            t0, T = BLOCKS[b]
-            qg[b] = sb.tile([P, 8 * E], BF16, name="qg", tag="qg", bufs=3, align_bytes=64)
-            for g in range(T // 2, T):
-                y = ps.tile([P, 512], F32, name="y", tag="y", bufs=3)
-                for j in range(4):
-                    m1_pass(b, y, P * j, j, g, P)
-                y_of[(b, g)] = y
+        def rg(b, unit):
+            g0, ng = unit
+            nc.vector.tensor_copy(
+                out=qg[b][:, E * g0 : E * (g0 + ng)].rearrange("p (c i j) -> p c j i", i=4, j=4),
+                in_=qp[(b, g0)][:].rearrange("p j (c i) -> p c j i", i=4),
+            )
 
-        def vd(b):
-            t0, T = BLOCKS[b]
-            for g in range(T // 2, T):
-                nc.vector.tensor_tensor(
-                    out=qg[b][:, E * g : E * g + E].rearrange("p (q j) -> p q j", j=4),
-                    in0=y_of[(b, g)][:].rearrange("p (j q) -> p q j", j=4),
-                    in1=b32[:].unsqueeze(1).to_broadcast([P, P, 4]),
-                    op=ALU.add,
-                )
+        def m1v(b, g):
+            y = ps.tile([P, 512], F32, name="y", tag="y", bufs=3)
+            for j in range(4):
+                m1_pass(b, y, P * j, j, g, P)
+            y_of[(b, g)] = y
 
-        def m2(b, h):
-            t0, T = BLOCKS[b]
+        def vd(b, g):
+            nc.vector.tensor_tensor(
+                out=qg[b][:, E * g : E * g + E].rearrange("p (q j) -> p q j", j=4),
+                in0=y_of[(b, g)][:].rearrange("p (j q) -> p q j", j=4),
+                in1=b32[:].unsqueeze(1).to_broadcast([P, P, 4]),
+                op=ALU.add,
+            )
+
+        def qq(b, h):
+            w = size(b) // 2
+            if h == 0:
+                c = sb.tile([P, 1024], U32, name="qc", tag="qc", bufs=2, align_bytes=64)
+                s = sb.tile([P, 1024], U8, name="qs", tag="qs", bufs=2, align_bytes=64)
+                qc[b] = (c, s)
+            c, s = qc[b]
+            nc.vector.quantize_mx(
+                out=c[:, P * w * h : P * w * (h + 1)].bitcast(FP8X4),
+                scales=s[:, P * w * h : P * w * (h + 1)],
+                in_=qg[b][:, E * w * h : E * w * (h + 1)],
+            )
+
+        def m2(b, h, part):
+            w = size(b) // 2
+            cut = (w + 1) // 2
+            lanes = range(0, cut) if part == 0 else range(cut, w)
             c, s = qc[b]
             c2, s2 = kc[b]
-            sc = ps.tile([P, 512], F32, name="sc", tag="sc", bufs=2)
-            for i in range(T // 2):
-                g = h * (T // 2) + i
+            if part == 0:
+                sc_of[(b, h)] = ps.tile([P, 512], F32, name="sc", tag="sc", bufs=1)
+            sc = sc_of[(b, h)]
+            for i in lanes:
+                g = h * w + i
                 nc.tensor.matmul_mx(
                     out=sc[:, P * i : P * i + P],
                     lhsT=c[:, P * g : P * g + P].bitcast(FP8X4),
@@ -280,13 +285,11 @@ def tile_dividedspacetimeattention_pa_t_kernel(tc, x, Wq, bq, k, out):
                     start=False,
                     stop=True,
                 )
-            sc_of[(b, h)] = sc
 
         def red(b, h):
-            t0, T = BLOCKS[b]
-            w = T // 2
+            w = size(b) // 2
             if h == 0:
-                s_sb[b] = sb.tile([P, 128], F32, name="s_sb", tag="s_sb", bufs=2)
+                s_sb[b] = sb.tile([P, 128], F32, name="s_sb", tag="s_sb", bufs=3)
             nc.vector.tensor_reduce(
                 out=s_sb[b][:, 16 * w * h : 16 * w * (h + 1)].rearrange("p (l g) -> p l g", g=16),
                 in_=sc_of[(b, h)][:, 0 : P * w].rearrange("p (l t g) -> p l g t", t=8, g=16),
@@ -295,12 +298,12 @@ def tile_dividedspacetimeattention_pa_t_kernel(tc, x, Wq, bq, k, out):
             )
 
         def shift(b):
-            t0, T = BLOCKS[b]
+            T = size(b)
             s3 = s_sb[b][:, 0 : 16 * T].rearrange("p (l g) -> p l g", g=16)
             mx = sb.tile([P, 8], F32, name="mx", tag="mx", bufs=2)
             nc.vector.tensor_reduce(out=mx[:, 0:T], in_=s3, axis=AX.X, op=ALU.max)
             d = sb.tile([P, 128], F32, name="d_sb", tag="d_sb", bufs=2)
-            nc.vector.tensor_tensor(
+            nc.gpsimd.tensor_tensor(
                 out=d[:, 0 : 16 * T].rearrange("p (l g) -> p l g", g=16),
                 in0=s3,
                 in1=mx[:, 0:T].unsqueeze(2).to_broadcast([P, T, 16]),
@@ -309,33 +312,25 @@ def tile_dividedspacetimeattention_pa_t_kernel(tc, x, Wq, bq, k, out):
             d_sb[b] = d
 
         def expo(b):
-            t0, T = BLOCKS[b]
+            T = size(b)
             ex = sb.tile([P, 128], F32, name="e_sb", tag="e_sb", bufs=2)
             nc.scalar.activation(
                 out=ex[:, 0 : 16 * T], in_=d_sb[b][:, 0 : 16 * T], func=ACT.Exp, scale=0.125
             )
             e_sb[b] = ex
 
-        def total(b):
+        def finish(b):
             t0, T = BLOCKS[b]
+            L = 8 // T
             e3 = e_sb[b][:, 0 : 16 * T].rearrange("p (l g) -> p l g", g=16)
             z = sb.tile([P, 8], F32, name="z", tag="z", bufs=2)
             nc.vector.tensor_reduce(out=z[:, 0:T], in_=e3, axis=AX.X, op=ALU.add)
             r = sb.tile([P, 8], F32, name="r", tag="r", bufs=2)
             nc.vector.reciprocal(out=r[:, 0:T], in_=z[:, 0:T])
-            r_sb[b] = r
-
-        def finish(b):
-            t0, T = BLOCKS[b]
-            L = 8 // T
-            e3 = e_sb[b][:, 0 : 16 * T].rearrange("p (l g) -> p l g", g=16)
             o = sb.tile([P, 128], F32, name="o_sb", tag="o_sb", bufs=3)
             o3 = o[:, 0 : 16 * T].rearrange("p (l g) -> p l g", g=16)
             nc.gpsimd.tensor_tensor(
-                out=o3,
-                in0=e3,
-                in1=r_sb[b][:, 0:T].unsqueeze(2).to_broadcast([P, T, 16]),
-                op=ALU.mult,
+                out=o3, in0=e3, in1=r[:, 0:T].unsqueeze(2).to_broadcast([P, T, 16]), op=ALU.mult
             )
             rows = ov[16 * t0 : 16 * (t0 + T), :, :].rearrange("r (h l) g -> l r h g", l=L)
             for l in range(L):
@@ -344,42 +339,89 @@ def tile_dividedspacetimeattention_pa_t_kernel(tc, x, Wq, bq, k, out):
         def ok(b):
             return 0 <= b < nb
 
-        t_x(0)
-        c_x(0)
-        t_k(0)
-        c_k(0)
-        for i in range(nb + 4):
-            if ok(i + 2):
-                load(i + 2)
-            if ok(i - 2):
-                quant(qg, i - 2, qc, "q", 2)
-            if ok(i - 1):
-                m1s(i - 1)
-            if ok(i - 2):
-                m2(i - 2, 0)
-                m2(i - 2, 1)
-            if ok(i):
-                quant(xg, i, xc, "x", 2)
-                quant(kg, i, kc, "k", 3)
-            if ok(i - 3):
-                expo(i - 3)
-            if ok(i + 1):
-                t_x(i + 1)
-                c_x(i + 1)
-            if ok(i - 3):
-                total(i - 3)
-                finish(i - 3)
-            if ok(i - 1):
-                rg(i - 1)
-            if ok(i):
-                m1v(i)
-            if ok(i - 2):
-                red(i - 2, 0)
-            if ok(i + 1):
-                t_k(i + 1)
-                c_k(i + 1)
-            if ok(i):
-                vd(i)
-            if ok(i - 2):
-                red(i - 2, 1)
-                shift(i - 2)
+        for w in ("x", "k"):
+            for m in range(4):
+                tp(0, w, m)
+            for m in range(4):
+                cp(0, w, m)
+        quant(xg, 0, xc, "x", 2)
+
+        for n in range(nb + 3):
+            a, b1, b2, nx = n, n - 1, n - 2, n + 1
+            ua = UNITS[size(a)] if ok(a) else None
+            u1 = UNITS[size(b1)] if ok(b1) else None
+            if ok(n + 2):
+                load(n + 2)
+            if ok(nx):
+                tp(nx, "x", 0)
+                tp(nx, "x", 1)
+            if ok(a):
+                qg[a] = sb.tile([P, 8 * E], BF16, name="qg", tag="qg", bufs=3, align_bytes=64)
+                m1s(a, ua[0], (0, 1))
+            if ok(b1):
+                m2(b1, 0, 0)
+            if ok(nx):
+                cp(nx, "x", 0)
+                cp(nx, "x", 1)
+            if ok(a):
+                act(a, ua[0], (0, 1))
+            if ok(b1):
+                for g in u1[2]:
+                    vd(b1, g)
+            if ok(b2):
+                red(b2, 1)
+            if ok(b1) and u1[1]:
+                rg(b1, u1[1])
+            if ok(a):
+                quant(kg, a, kc, "k", 3)
+            if ok(b1):
+                qq(b1, 1)
+            if ok(b2):
+                shift(b2)
+            if ok(nx):
+                tp(nx, "x", 2)
+                tp(nx, "x", 3)
+            if ok(a):
+                m1s(a, ua[0], (2, 3))
+            if ok(b1):
+                m2(b1, 0, 1)
+            if ok(nx):
+                cp(nx, "x", 2)
+                cp(nx, "x", 3)
+            if ok(a):
+                act(a, ua[0], (2, 3))
+            if ok(b2):
+                expo(b2)
+            if ok(b1):
+                red(b1, 0)
+            if ok(nx):
+                tp(nx, "k", 0)
+                tp(nx, "k", 1)
+            if ok(a) and ua[1]:
+                m1s(a, ua[1], (0, 1, 2, 3))
+            if ok(b1):
+                m2(b1, 1, 0)
+            if ok(nx):
+                cp(nx, "k", 0)
+                cp(nx, "k", 1)
+            if ok(a) and ua[1]:
+                act(a, ua[1], (0, 1, 2, 3))
+            if ok(a):
+                rg(a, ua[0])
+            if ok(nx):
+                quant(xg, nx, xc, "x", 2)
+            if ok(a):
+                qq(a, 0)
+            if ok(b2):
+                finish(b2)
+            if ok(nx):
+                tp(nx, "k", 2)
+                tp(nx, "k", 3)
+            if ok(a):
+                for g in ua[2]:
+                    m1v(a, g)
+            if ok(b1):
+                m2(b1, 1, 1)
+            if ok(nx):
+                cp(nx, "k", 2)
+                cp(nx, "k", 3)

from contextlib import ExitStack

import concourse.mybir as mybir
from concourse.masks import make_identity

F32 = mybir.dt.float32
BF16 = mybir.dt.bfloat16
U32 = mybir.dt.uint32
U8 = mybir.dt.uint8
FP8X4 = mybir.dt.float8_e4m3fn_x4
ALU = mybir.AluOpType
ACT = mybir.ActivationFunctionType
AX = mybir.AxisListType

P = 128
E = 512
STEPS = 98
FLOPS = 2 * 12544 * 512 * 512 + 2 * 784 * 16 * 16 * 512
BIG = 2.0 ** 100

BLOCKS = [(0, 2), (2, 4)] + [(6 + 8 * i, 8) for i in range(11)] + [(94, 4)]
UNITS = {8: ((0, 4), (4, 2), (6, 7)), 4: ((0, 2), None, (2, 3)), 2: ((0, 1), None, (1,))}


def tile_dividedspacetimeattention_pa_t_kernel(tc, x, Wq, bq, k, out):
    nc = tc.nc
    nb = len(BLOCKS)
    xv = x.rearrange("b (q t) e -> (b q) t e", t=STEPS)
    kv = k.rearrange("b h (j t) g e -> (t g) (b h j) e", j=2, t=STEPS)
    ov = out.rearrange("b h (j t) f g -> (t f) (b h j) g", j=2, t=STEPS)

    with ExitStack() as ctx:
        const = ctx.enter_context(tc.tile_pool(name="const", bufs=1))
        sb = ctx.enter_context(tc.tile_pool(name="sb", bufs=2))
        ps = ctx.enter_context(tc.psum_pool(name="ps", bufs=1))
        ctx.enter_context(tc.manual_schedule())

        x_sb = {}
        k_sb = {}
        xg = {}
        kg = {}
        xc = {}
        kc = {}
        qp = {}
        qg = {}
        qc = {}
        s_sb = {}
        d_sb = {}
        e_sb = {}
        r_sb = {}
        tr_of = {}
        y_of = {}
        sc_of = {}

        def load(b):
            t0, T = BLOCKS[b]
            L = 8 // T
            xt = sb.tile([P, 8 * E], BF16, name="x_sb", tag="x_sb", bufs=3)
            nc.sync.dma_start(
                out=xt[:, 0 : E * T].rearrange("p (t e) -> p t e", e=E),
                in_=xv[:, t0 : t0 + T, :],
            )
            x_sb[b] = xt
            kt = sb.tile([P, 8 * E], BF16, name="k_sb", tag="k_sb", bufs=3)
            k3 = kt[:, 0 : E * T].rearrange("p (h e) -> p h e", e=E)
            rows = kv[16 * t0 : 16 * (t0 + T), :, :].rearrange("r (h l) e -> l r h e", l=L)
            for l in range(L):
                nc.sync.dma_start(out=k3[16 * T * l : 16 * T * (l + 1), :, :], in_=rows[l])
            k_sb[b] = kt

        load(0)
        wraw = const.tile([P, 4, E], BF16, name="wraw")
        for u in range(2):
            nc.sync.dma_start(
                out=wraw[:, 2 * u : 2 * u + 2, :],
                in_=Wq[256 * u : 256 * u + 256, :].rearrange("(p e) n -> p e n", e=2),
            )
        b_bf = const.tile([P, 4], BF16, name="b_bf")
        nc.scalar.dma_start(
            out=b_bf[:].rearrange("p (u e) -> p u e", u=2),
            in_=bq.rearrange("(u p e) -> p u e", u=2, e=2),
        )
        load(1)

        ident = const.tile([P, P], F32, name="ident")
        make_identity(nc, ident[:])
        zero = const.tile([P, 8], F32, name="zero")
        nc.vector.memset(zero[:], 0.0)
        warm = const.tile([P, 8], F32, name="warm")
        nc.scalar.activation(out=warm[:], in_=zero[:], func=ACT.Exp)

        perm = const.tile([P, P], F32, name="perm")
        nc.vector.tensor_copy(
            out=perm[:].rearrange("p (b j f) -> p b j f", b=4, j=2, f=16),
            in_=ident[:].rearrange("p (b f j) -> p b j f", b=4, f=16, j=2),
        )
        ag = const.tile([P, 4 * P], BF16, name="ag", align_bytes=64)
        bg = const.tile([P, 4 * P], BF16, name="bg", align_bytes=64)
        nc.vector.memset(ag[:], 0.0)
        nc.vector.memset(bg[:], 0.0)
        slot = ident[:, 0:8].unsqueeze(2).to_broadcast([P, 8, 16])
        nc.vector.tensor_copy(
            out=ag[:].rearrange("p (s f j) -> p s f j", s=8, f=16, j=4)[:, :, :, 0], in_=slot
        )
        nc.vector.tensor_scalar(
            out=bg[:].rearrange("p (s f j) -> p s f j", s=8, f=16, j=4)[:, :, :, 0],
            in0=slot,
            scalar1=-1.0,
            scalar2=BIG,
            op0=ALU.add,
            op1=ALU.mult,
        )
        ac = const.tile([P, P], U32, name="ac", align_bytes=64)
        asc = const.tile([P, P], U8, name="asc", align_bytes=64)
        bc = const.tile([P, P], U32, name="bc", align_bytes=64)
        bsc = const.tile([P, P], U8, name="bsc", align_bytes=64)
        nc.vector.quantize_mx(out=ac[:].bitcast(FP8X4), scales=asc[:], in_=ag[:])
        nc.vector.quantize_mx(out=bc[:].bitcast(FP8X4), scales=bsc[:], in_=bg[:])

        b32 = const.tile([P, 4], F32, name="b32")
        nc.vector.tensor_copy(out=b32[:], in_=b_bf[:])
        wg = const.tile([P, 4 * E], BF16, name="wg", align_bytes=64)
        wgv = wg[:].rearrange("p (u e m j) -> p u e m j", u=2, e=2, m=P, j=4)
        wrv = wraw[:].rearrange("p j (u m e) -> p u e m j", u=2, m=P, e=2)
        for u in range(2):
            for e in range(2):
                nc.vector.tensor_copy(out=wgv[:, u, e], in_=wrv[:, u, e])
        wc = const.tile([P, E], U32, name="wc", align_bytes=64)
        ws = const.tile([P, E], U8, name="ws", align_bytes=64)
        nc.vector.quantize_mx(out=wc[:].bitcast(FP8X4), scales=ws[:], in_=wg[:])

        def size(b):
            return BLOCKS[b][1]

        def tp(b, w, m):
            T = size(b)
            if m >= T // 2:
                return
            tr = ps.tile([P, 512], F32, name="tr", tag="tr", bufs=4)
            if w == "x":
                src = x_sb[b][:].bitcast(F32)
                trv = tr[:].rearrange("p (u c s f) -> p u c s f", u=2, c=8, s=2, f=16)
            else:
                src = k_sb[b][:].bitcast(F32)
            for s in range(2):
                for u in range(2):
                    c0 = 256 * (2 * m + s) + 128 * u
                    if w == "x":
                        nc.tensor.transpose(trv[:, u, :, s, :], src[:, c0 : c0 + 128], perm[:])
                    else:
                        o = 256 * s + 128 * u
                        nc.tensor.transpose(tr[:, o : o + 128], src[:, c0 : c0 + 128], ident[:])
            tr_of[(w, b, m)] = tr

        def cp(b, w, m):
            T = size(b)
            if m >= T // 2:
                return
            if w == "x":
                if m == 0:
                    xg[b] = sb.tile([P, 8 * E], BF16, name="xg", tag="xg", bufs=2, align_bytes=64)
                gv = xg[b][:].bitcast(F32)[:, 0 : 256 * T].rearrange(
                    "p (c m q u) -> p c m q u", c=8, m=T // 2, q=32, u=2
                )
                nc.scalar.copy(
                    out=gv[:, :, m, :, :],
                    in_=tr_of[(w, b, m)][:].rearrange("p (u c q) -> p c q u", u=2, c=8, q=32),
                )
            else:
                if m == 0:
                    kg[b] = sb.tile([P, 8 * E], BF16, name="kg", tag="kg", bufs=2, align_bytes=64)
                nc.scalar.copy(
                    out=kg[b][:].bitcast(F32)[:, 512 * m : 512 * m + 512].rearrange(
                        "p (s q u) -> p s q u", s=2, q=P, u=2
                    ),
                    in_=tr_of[(w, b, m)][:].rearrange("p (s u q) -> p s q u", s=2, u=2, q=P),
                )

        def quant(src, b, store, tag, bufs):
            T = size(b)
            c = sb.tile([P, 1024], U32, name=tag + "c", tag=tag + "c", bufs=bufs, align_bytes=64)
            s = sb.tile([P, 1024], U8, name=tag + "s", tag=tag + "s", bufs=bufs, align_bytes=64)
            nc.vector.quantize_mx(
                out=c[:, 0 : P * T].bitcast(FP8X4), scales=s[:, 0 : P * T], in_=src[b][:, 0 : E * T]
            )
            store[b] = (c, s)

        def m1_pass(b, y, o, j, g0, n):
            c, s = xc[b]
            nc.tensor.matmul_mx(
                out=y[:, o : o + n],
                lhsT=wc[:, P * j : P * j + P].bitcast(FP8X4),
                lhsT_scale=ws[:, P * j : P * j + P],
                rhs=c[:, P * g0 : P * g0 + n].bitcast(FP8X4),
                rhs_scale=s[:, P * g0 : P * g0 + n],
                start=True,
                stop=True,
            )

        def m1s(b, unit, js):
            g0, ng = unit
            n = P * ng
            per = 512 // n
            for j in js:
                if j % per == 0:
                    y_of[(b, g0, j // per)] = ps.tile([P, 512], F32, name="y", tag="y", bufs=3)
                m1_pass(b, y_of[(b, g0, j // per)], n * (j % per), j, g0, n)

        def act(b, unit, js):
            g0, ng = unit
            n = P * ng
            per = 512 // n
            for j in js:
                if j == 0:
                    qp[(b, g0)] = sb.tile([P, 4, n], BF16, name="qp%d" % ng, tag="qp%d" % ng, bufs=2)
                o = n * (j % per)
                nc.scalar.activation(
                    out=qp[(b, g0)][:, j, :],
                    in_=y_of[(b, g0, j // per)][:, o : o + n],
                    func=ACT.Identity,
                    bias=b32[:, j : j + 1],
                    scale=1.0,
                )

        def rg(b, unit):
            g0, ng = unit
            nc.vector.tensor_copy(
                out=qg[b][:, E * g0 : E * (g0 + ng)].rearrange("p (c i j) -> p c j i", i=4, j=4),
                in_=qp[(b, g0)][:].rearrange("p j (c i) -> p c j i", i=4),
            )

        def m1v(b, g):
            y = ps.tile([P, 512], F32, name="y", tag="y", bufs=3)
            for j in range(4):
                m1_pass(b, y, P * j, j, g, P)
            y_of[(b, g)] = y

        def vd(b, g):
            nc.vector.tensor_tensor(
                out=qg[b][:, E * g : E * g + E].rearrange("p (q j) -> p q j", j=4),
                in0=y_of[(b, g)][:].rearrange("p (j q) -> p q j", j=4),
                in1=b32[:].unsqueeze(1).to_broadcast([P, P, 4]),
                op=ALU.add,
            )

        def qq(b, h):
            w = size(b) // 2
            if h == 0:
                c = sb.tile([P, 1024], U32, name="qc", tag="qc", bufs=2, align_bytes=64)
                s = sb.tile([P, 1024], U8, name="qs", tag="qs", bufs=2, align_bytes=64)
                qc[b] = (c, s)
            c, s = qc[b]
            nc.vector.quantize_mx(
                out=c[:, P * w * h : P * w * (h + 1)].bitcast(FP8X4),
                scales=s[:, P * w * h : P * w * (h + 1)],
                in_=qg[b][:, E * w * h : E * w * (h + 1)],
            )

        def m2(b, h, part):
            w = size(b) // 2
            cut = (w + 1) // 2
            lanes = range(0, cut) if part == 0 else range(cut, w)
            c, s = qc[b]
            c2, s2 = kc[b]
            if part == 0:
                sc_of[(b, h)] = ps.tile([P, 512], F32, name="sc", tag="sc", bufs=1)
            sc = sc_of[(b, h)]
            for i in lanes:
                g = h * w + i
                nc.tensor.matmul_mx(
                    out=sc[:, P * i : P * i + P],
                    lhsT=c[:, P * g : P * g + P].bitcast(FP8X4),
                    lhsT_scale=s[:, P * g : P * g + P],
                    rhs=c2[:, P * g : P * g + P].bitcast(FP8X4),
                    rhs_scale=s2[:, P * g : P * g + P],
                    start=True,
                    stop=False,
                )
                nc.tensor.matmul_mx(
                    out=sc[:, P * i : P * i + P],
                    lhsT=ac[:].bitcast(FP8X4),
                    lhsT_scale=asc[:],
                    rhs=bc[:].bitcast(FP8X4),
                    rhs_scale=bsc[:],
                    start=False,
                    stop=True,
                )

        def red(b, h):
            w = size(b) // 2
            if h == 0:
                s_sb[b] = sb.tile([P, 128], F32, name="s_sb", tag="s_sb", bufs=3)
            nc.vector.tensor_reduce(
                out=s_sb[b][:, 16 * w * h : 16 * w * (h + 1)].rearrange("p (l g) -> p l g", g=16),
                in_=sc_of[(b, h)][:, 0 : P * w].rearrange("p (l t g) -> p l g t", t=8, g=16),
                axis=AX.X,
                op=ALU.max,
            )

        def shift(b):
            T = size(b)
            s3 = s_sb[b][:, 0 : 16 * T].rearrange("p (l g) -> p l g", g=16)
            mx = sb.tile([P, 8], F32, name="mx", tag="mx", bufs=2)
            nc.vector.tensor_reduce(out=mx[:, 0:T], in_=s3, axis=AX.X, op=ALU.max)
            d = sb.tile([P, 128], F32, name="d_sb", tag="d_sb", bufs=2)
            nc.gpsimd.tensor_tensor(
                out=d[:, 0 : 16 * T].rearrange("p (l g) -> p l g", g=16),
                in0=s3,
                in1=mx[:, 0:T].unsqueeze(2).to_broadcast([P, T, 16]),
                op=ALU.subtract,
            )
            d_sb[b] = d

        def expo(b):
            T = size(b)
            ex = sb.tile([P, 128], F32, name="e_sb", tag="e_sb", bufs=2)
            nc.scalar.activation(
                out=ex[:, 0 : 16 * T], in_=d_sb[b][:, 0 : 16 * T], func=ACT.Exp, scale=0.125
            )
            e_sb[b] = ex

        def finish(b):
            t0, T = BLOCKS[b]
            L = 8 // T
            e3 = e_sb[b][:, 0 : 16 * T].rearrange("p (l g) -> p l g", g=16)
            z = sb.tile([P, 8], F32, name="z", tag="z", bufs=2)
            nc.vector.tensor_reduce(out=z[:, 0:T], in_=e3, axis=AX.X, op=ALU.add)
            r = sb.tile([P, 8], F32, name="r", tag="r", bufs=2)
            nc.vector.reciprocal(out=r[:, 0:T], in_=z[:, 0:T])
            o = sb.tile([P, 128], F32, name="o_sb", tag="o_sb", bufs=3)
            o3 = o[:, 0 : 16 * T].rearrange("p (l g) -> p l g", g=16)
            nc.gpsimd.tensor_tensor(
                out=o3, in0=e3, in1=r[:, 0:T].unsqueeze(2).to_broadcast([P, T, 16]), op=ALU.mult
            )
            rows = ov[16 * t0 : 16 * (t0 + T), :, :].rearrange("r (h l) g -> l r h g", l=L)
            for l in range(L):
                nc.sync.dma_start(out=rows[l], in_=o3[16 * T * l : 16 * T * (l + 1), :, :])

        def ok(b):
            return 0 <= b < nb

        for w in ("x", "k"):
            for m in range(4):
                tp(0, w, m)
            for m in range(4):
                cp(0, w, m)
        quant(xg, 0, xc, "x", 2)

        for n in range(nb + 3):
            a, b1, b2, nx = n, n - 1, n - 2, n + 1
            ua = UNITS[size(a)] if ok(a) else None
            u1 = UNITS[size(b1)] if ok(b1) else None
            if ok(n + 2):
                load(n + 2)
            if ok(nx):
                tp(nx, "x", 0)
                tp(nx, "x", 1)
            if ok(a):
                qg[a] = sb.tile([P, 8 * E], BF16, name="qg", tag="qg", bufs=3, align_bytes=64)
                m1s(a, ua[0], (0, 1))
            if ok(b1):
                m2(b1, 0, 0)
            if ok(nx):
                cp(nx, "x", 0)
                cp(nx, "x", 1)
            if ok(a):
                act(a, ua[0], (0, 1))
            if ok(b1):
                for g in u1[2]:
                    vd(b1, g)
            if ok(b2):
                red(b2, 1)
            if ok(b1) and u1[1]:
                rg(b1, u1[1])
            if ok(a):
                quant(kg, a, kc, "k", 3)
            if ok(b1):
                qq(b1, 1)
            if ok(b2):
                shift(b2)
            if ok(nx):
                tp(nx, "x", 2)
                tp(nx, "x", 3)
            if ok(a):
                m1s(a, ua[0], (2, 3))
            if ok(b1):
                m2(b1, 0, 1)
            if ok(nx):
                cp(nx, "x", 2)
                cp(nx, "x", 3)
            if ok(a):
                act(a, ua[0], (2, 3))
            if ok(b2):
                expo(b2)
            if ok(b1):
                red(b1, 0)
            if ok(nx):
                tp(nx, "k", 0)
                tp(nx, "k", 1)
            if ok(a) and ua[1]:
                m1s(a, ua[1], (0, 1, 2, 3))
            if ok(b1):
                m2(b1, 1, 0)
            if ok(nx):
                cp(nx, "k", 0)
                cp(nx, "k", 1)
            if ok(a) and ua[1]:
                act(a, ua[1], (0, 1, 2, 3))
            if ok(a):
                rg(a, ua[0])
            if ok(nx):
                quant(xg, nx, xc, "x", 2)
            if ok(a):
                qq(a, 0)
            if ok(b2):
                finish(b2)
            if ok(nx):
                tp(nx, "k", 2)
                tp(nx, "k", 3)
            if ok(a):
                for g in ua[2]:
                    m1v(a, g)
            if ok(b1):
                m2(b1, 1, 1)
            if ok(nx):
                cp(nx, "k", 2)
                cp(nx, "k", 3)
